import numpy as np
import ml_dtypes

BF16 = ml_dtypes.bfloat16


def bf(x):
    return np.asarray(x, np.float32).astype(BF16)


def f32(x):
    return np.asarray(x, np.float32)


def f64(x):
    return np.asarray(x).astype(np.float64)


def striped(idx):
    return np.tile(idx.reshape(-1, 16).T, (8, 1))


C, S, N = 128, 512, 256
EPS = 1e-6


def setup_inputs():
    bank = np.random.standard_normal((C, S))
    bank = bank / np.linalg.norm(bank, axis=0, keepdims=True)
    return {"base": f32(bank), "embeds": f32(0.3 * np.random.standard_normal((C, N))), "offs": striped(np.random.permutation(S)[:N])}


def reference(base, embeds, offs):
    idx = offs[:16].T.reshape(-1)
    x = f64(embeds)
    rinv = 1.0 / (np.sqrt(np.sum(x * x, axis=0, keepdims=True)) + EPS)
    res = f64(base).copy()
    res[:, idx] = x * rinv
    return res

@@ -1,0 +1,45 @@
+import concourse.mybir as mybir
+
+F32 = mybir.dt.float32
+BF16 = mybir.dt.bfloat16
+U16 = mybir.dt.uint16
+MULT = mybir.AluOpType.mult
+SQRT = mybir.ActivationFunctionType.Sqrt
+
+C = 128
+S = 512
+N = 256
+EPS = 1e-6
+
+FLOPS = 2 * C * N
+
+
+def tile_clusterator_kernel(tc, base, embeds, offs, out):
+    nc = tc.nc
+    with (
+        tc.tile_pool(name="held", bufs=1) as held,
+        tc.psum_pool(name="psum", bufs=1) as psum,
+    ):
+        offsets = held.tile([C, N // 16], U16, name="offsets")
+        nc.sync.dma_start(offsets[:], offs)
+        new = held.tile([C, N], F32, name="new")
+        nc.scalar.dma_start(new[:], embeds)
+        bank = held.tile([C, S], F32, name="bank")
+        nc.sync.dma_start(bank[:], base)
+
+        ones = held.tile([C, C], BF16, name="ones")
+        nc.vector.memset(ones[:], 1.0)
+        squares = held.tile([C, N], BF16, name="squares")
+        nc.vector.tensor_tensor(squares[:], new[:], new[:], MULT)
+        sums = psum.tile([C, N], F32, name="sums")
+        nc.tensor.matmul(sums[:], ones[:], squares[:], start=True, stop=True)
+
+        norm = held.tile([C, N], F32, name="norm")
+        nc.scalar.activation(norm[:], sums[:], SQRT)
+        padded = held.tile([C, N], F32, name="padded")
+        nc.vector.tensor_scalar_add(padded[:], norm[:], EPS)
+        rinv = held.tile([C, N], F32, name="rinv")
+        nc.vector.reciprocal(rinv[:], padded[:])
+
+        nc.vector.tensor_tensor(bank[:].indirect(offsets[:]), new[:], rinv[:], MULT)
+        nc.sync.dma_start(out, bank[:])

@@ -5,6 +5,8 @@ BF16 = mybir.dt.bfloat16
 U16 = mybir.dt.uint16
 MULT = mybir.AluOpType.mult
 SQRT = mybir.ActivationFunctionType.Sqrt
+SQUARE = mybir.ActivationFunctionType.Square
+RSQRT = mybir.ActivationFunctionType.Abs_reciprocal_sqrt
 
 C = 128
 S = 512
@@ -36,10 +38,10 @@ def tile_clusterator_kernel(tc, base, embeds, offs, out):
 
         norm = held.tile([C, N], F32, name="norm")
         nc.scalar.activation(norm[:], sums[:], SQRT)
-        padded = held.tile([C, N], F32, name="padded")
-        nc.vector.tensor_scalar_add(padded[:], norm[:], EPS)
+        padded_sq = held.tile([C, N], F32, name="padded_sq")
+        nc.scalar.activation(padded_sq[:], norm[:], SQUARE, bias=EPS)
         rinv = held.tile([C, N], F32, name="rinv")
-        nc.vector.reciprocal(rinv[:], padded[:])
+        nc.scalar.activation(rinv[:], padded_sq[:], RSQRT)
 
         nc.vector.tensor_tensor(bank[:].indirect(offsets[:]), new[:], rinv[:], MULT)
         nc.sync.dma_start(out, bank[:])

@@ -4,7 +4,6 @@ F32 = mybir.dt.float32
 BF16 = mybir.dt.bfloat16
 U16 = mybir.dt.uint16
 MULT = mybir.AluOpType.mult
-SQRT = mybir.ActivationFunctionType.Sqrt
 SQUARE = mybir.ActivationFunctionType.Square
 RSQRT = mybir.ActivationFunctionType.Abs_reciprocal_sqrt
 
@@ -12,6 +11,7 @@ C = 128
 S = 512
 N = 256
 EPS = 1e-6
+TINY = 1e-30
 
 FLOPS = 2 * C * N
 
@@ -36,8 +36,10 @@ def tile_clusterator_kernel(tc, base, embeds, offs, out):
         sums = psum.tile([C, N], F32, name="sums")
         nc.tensor.matmul(sums[:], ones[:], squares[:], start=True, stop=True)
 
+        rough = held.tile([C, N], F32, name="rough")
+        nc.scalar.activation(rough[:], sums[:], RSQRT, bias=TINY)
         norm = held.tile([C, N], F32, name="norm")
-        nc.scalar.activation(norm[:], sums[:], SQRT)
+        nc.vector.tensor_tensor(norm[:], sums[:], rough[:], MULT)
         padded_sq = held.tile([C, N], F32, name="padded_sq")
         nc.scalar.activation(padded_sq[:], norm[:], SQUARE, bias=EPS)
         rinv = held.tile([C, N], F32, name="rinv")

@@ -12,6 +12,8 @@ S = 512
 N = 256
 EPS = 1e-6
 TINY = 1e-30
+PIECE = N // 2
+PIECES = range(N // PIECE)
 
 FLOPS = 2 * C * N
 
@@ -28,22 +30,27 @@ def tile_clusterator_kernel(tc, base, embeds, offs, out):
         nc.scalar.dma_start(new[:], embeds)
         bank = held.tile([C, S], F32, name="bank")
         nc.sync.dma_start(bank[:], base)
+        new_piece = [new[:, p * PIECE : (p + 1) * PIECE] for p in PIECES]
 
         ones = held.tile([C, C], BF16, name="ones")
         nc.vector.memset(ones[:], 1.0)
-        squares = held.tile([C, N], BF16, name="squares")
-        nc.vector.tensor_tensor(squares[:], new[:], new[:], MULT)
-        sums = psum.tile([C, N], F32, name="sums")
-        nc.tensor.matmul(sums[:], ones[:], squares[:], start=True, stop=True)
+        squares = [held.tile([C, PIECE], BF16, name=f"squares{p}") for p in PIECES]
+        sums = [psum.tile([C, PIECE], F32, name=f"sums{p}") for p in PIECES]
+        for p in PIECES:
+            nc.vector.tensor_tensor(squares[p][:], new_piece[p], new_piece[p], MULT)
+            nc.tensor.matmul(sums[p][:], ones[:], squares[p][:], start=True, stop=True)
 
-        rough = held.tile([C, N], F32, name="rough")
-        nc.scalar.activation(rough[:], sums[:], RSQRT, bias=TINY)
-        norm = held.tile([C, N], F32, name="norm")
-        nc.vector.tensor_tensor(norm[:], sums[:], rough[:], MULT)
-        padded_sq = held.tile([C, N], F32, name="padded_sq")
-        nc.scalar.activation(padded_sq[:], norm[:], SQUARE, bias=EPS)
-        rinv = held.tile([C, N], F32, name="rinv")
-        nc.scalar.activation(rinv[:], padded_sq[:], RSQRT)
+        rough = [held.tile([C, PIECE], F32, name=f"rough{p}") for p in PIECES]
+        norm = [held.tile([C, PIECE], F32, name=f"norm{p}") for p in PIECES]
+        for p in PIECES:
+            nc.scalar.activation(rough[p][:], sums[p][:], RSQRT, bias=TINY)
+            nc.vector.tensor_tensor(norm[p][:], sums[p][:], rough[p][:], MULT)
 
-        nc.vector.tensor_tensor(bank[:].indirect(offsets[:]), new[:], rinv[:], MULT)
+        padded_sq = [held.tile([C, PIECE], F32, name=f"padded_sq{p}") for p in PIECES]
+        rinv = [held.tile([C, PIECE], F32, name=f"rinv{p}") for p in PIECES]
+        for p in PIECES:
+            nc.scalar.activation(padded_sq[p][:], norm[p][:], SQUARE, bias=EPS)
+            nc.scalar.activation(rinv[p][:], padded_sq[p][:], RSQRT)
+            piece_offsets = offsets[:, p * (PIECE // 16) : (p + 1) * (PIECE // 16)]
+            nc.vector.tensor_tensor(bank[:].indirect(piece_offsets), new_piece[p], rinv[p][:], MULT)
         nc.sync.dma_start(out, bank[:])

@@ -4,7 +4,7 @@ F32 = mybir.dt.float32
 BF16 = mybir.dt.bfloat16
 U16 = mybir.dt.uint16
 MULT = mybir.AluOpType.mult
-SQUARE = mybir.ActivationFunctionType.Square
+ADD = mybir.AluOpType.add
 RSQRT = mybir.ActivationFunctionType.Abs_reciprocal_sqrt
 
 C = 128
@@ -12,7 +12,8 @@ S = 512
 N = 256
 EPS = 1e-6
 TINY = 1e-30
-PIECE = N // 2
+SHRINK = 2.0**-19
+PIECE = N // 4
 PIECES = range(N // PIECE)
 
 FLOPS = 2 * C * N
@@ -24,33 +25,32 @@ def tile_clusterator_kernel(tc, base, embeds, offs, out):
         tc.tile_pool(name="held", bufs=1) as held,
         tc.psum_pool(name="psum", bufs=1) as psum,
     ):
+        new = held.tile([C, N], F32, name="new")
+        nc.sync.dma_start(new[:, 0 : N // 2], embeds[:, 0 : N // 2])
+        nc.scalar.dma_start(new[:, N // 2 : N], embeds[:, N // 2 : N])
         offsets = held.tile([C, N // 16], U16, name="offsets")
         nc.sync.dma_start(offsets[:], offs)
-        new = held.tile([C, N], F32, name="new")
-        nc.scalar.dma_start(new[:], embeds)
         bank = held.tile([C, S], F32, name="bank")
         nc.sync.dma_start(bank[:], base)
         new_piece = [new[:, p * PIECE : (p + 1) * PIECE] for p in PIECES]
 
-        ones = held.tile([C, C], BF16, name="ones")
-        nc.vector.memset(ones[:], 1.0)
+        weights = held.tile([C, C], BF16, name="weights")
+        nc.vector.memset(weights[:], SHRINK)
         squares = [held.tile([C, PIECE], BF16, name=f"squares{p}") for p in PIECES]
         sums = [psum.tile([C, PIECE], F32, name=f"sums{p}") for p in PIECES]
         for p in PIECES:
             nc.vector.tensor_tensor(squares[p][:], new_piece[p], new_piece[p], MULT)
-            nc.tensor.matmul(sums[p][:], ones[:], squares[p][:], start=True, stop=True)
+            nc.tensor.matmul(sums[p][:], weights[:], squares[p][:], start=True, stop=True)
 
         rough = [held.tile([C, PIECE], F32, name=f"rough{p}") for p in PIECES]
-        norm = [held.tile([C, PIECE], F32, name=f"norm{p}") for p in PIECES]
+        bracket = [held.tile([C, PIECE], F32, name=f"bracket{p}") for p in PIECES]
+        rinv = held.tile([C, N], F32, name="rinv")
         for p in PIECES:
-            nc.scalar.activation(rough[p][:], sums[p][:], RSQRT, bias=TINY)
-            nc.vector.tensor_tensor(norm[p][:], sums[p][:], rough[p][:], MULT)
+            nc.scalar.activation(rough[p][:], sums[p][:], RSQRT, bias=TINY, scale=1.0 / SHRINK)
+            nc.vector.scalar_tensor_tensor(bracket[p][:], rough[p][:], 1.0 / (2.0 * EPS), sums[p][:], ADD, MULT)
+            nc.scalar.activation(
+                rinv[:, p * PIECE : (p + 1) * PIECE], bracket[p][:], RSQRT, bias=EPS * EPS, scale=2.0 * EPS / SHRINK
+            )
 
-        padded_sq = [held.tile([C, PIECE], F32, name=f"padded_sq{p}") for p in PIECES]
-        rinv = [held.tile([C, PIECE], F32, name=f"rinv{p}") for p in PIECES]
-        for p in PIECES:
-            nc.scalar.activation(padded_sq[p][:], norm[p][:], SQUARE, bias=EPS)
-            nc.scalar.activation(rinv[p][:], padded_sq[p][:], RSQRT)
-            piece_offsets = offsets[:, p * (PIECE // 16) : (p + 1) * (PIECE // 16)]
-            nc.vector.tensor_tensor(bank[:].indirect(piece_offsets), new_piece[p], rinv[p][:], MULT)
+        nc.vector.tensor_tensor(bank[:].indirect(offsets[:]), new[:], rinv[:], MULT)
         nc.sync.dma_start(out, bank[:])

@@ -13,7 +13,7 @@ N = 256
 EPS = 1e-6
 TINY = 1e-30
 SHRINK = 2.0**-19
-PIECE = N // 4
+PIECE = N // 8
 PIECES = range(N // PIECE)
 
 FLOPS = 2 * C * N

@@ -28,10 +28,10 @@ def tile_clusterator_kernel(tc, base, embeds, offs, out):
         new = held.tile([C, N], F32, name="new")
         nc.sync.dma_start(new[:, 0 : N // 2], embeds[:, 0 : N // 2])
         nc.scalar.dma_start(new[:, N // 2 : N], embeds[:, N // 2 : N])
-        offsets = held.tile([C, N // 16], U16, name="offsets")
-        nc.sync.dma_start(offsets[:], offs)
         bank = held.tile([C, S], F32, name="bank")
         nc.sync.dma_start(bank[:], base)
+        offsets = held.tile([C, N // 16], U16, name="offsets")
+        nc.sync.dma_start(offsets[:], offs)
         new_piece = [new[:, p * PIECE : (p + 1) * PIECE] for p in PIECES]
 
         weights = held.tile([C, C], BF16, name="weights")

import concourse.mybir as mybir

F32 = mybir.dt.float32
BF16 = mybir.dt.bfloat16
U16 = mybir.dt.uint16
MULT = mybir.AluOpType.mult
ADD = mybir.AluOpType.add
RSQRT = mybir.ActivationFunctionType.Abs_reciprocal_sqrt

C = 128
S = 512
N = 256
EPS = 1e-6
TINY = 1e-30
SHRINK = 2.0**-19
PIECE = N // 8
PIECES = range(N // PIECE)

FLOPS = 2 * C * N


def tile_clusterator_kernel(tc, base, embeds, offs, out):
    nc = tc.nc
    with (
        tc.tile_pool(name="held", bufs=1) as held,
        tc.psum_pool(name="psum", bufs=1) as psum,
    ):
        new = held.tile([C, N], F32, name="new")
        nc.sync.dma_start(new[:, 0 : N // 2], embeds[:, 0 : N // 2])
        nc.scalar.dma_start(new[:, N // 2 : N], embeds[:, N // 2 : N])
        bank = held.tile([C, S], F32, name="bank")
        nc.sync.dma_start(bank[:], base)
        offsets = held.tile([C, N // 16], U16, name="offsets")
        nc.sync.dma_start(offsets[:], offs)
        new_piece = [new[:, p * PIECE : (p + 1) * PIECE] for p in PIECES]

        weights = held.tile([C, C], BF16, name="weights")
        nc.vector.memset(weights[:], SHRINK)
        squares = [held.tile([C, PIECE], BF16, name=f"squares{p}") for p in PIECES]
        sums = [psum.tile([C, PIECE], F32, name=f"sums{p}") for p in PIECES]
        for p in PIECES:
            nc.vector.tensor_tensor(squares[p][:], new_piece[p], new_piece[p], MULT)
            nc.tensor.matmul(sums[p][:], weights[:], squares[p][:], start=True, stop=True)

        rough = [held.tile([C, PIECE], F32, name=f"rough{p}") for p in PIECES]
        bracket = [held.tile([C, PIECE], F32, name=f"bracket{p}") for p in PIECES]
        rinv = held.tile([C, N], F32, name="rinv")
        for p in PIECES:
            nc.scalar.activation(rough[p][:], sums[p][:], RSQRT, bias=TINY, scale=1.0 / SHRINK)
            nc.vector.scalar_tensor_tensor(bracket[p][:], rough[p][:], 1.0 / (2.0 * EPS), sums[p][:], ADD, MULT)
            nc.scalar.activation(
                rinv[:, p * PIECE : (p + 1) * PIECE], bracket[p][:], RSQRT, bias=EPS * EPS, scale=2.0 * EPS / SHRINK
            )

        nc.vector.tensor_tensor(bank[:].indirect(offsets[:]), new[:], rinv[:], MULT)
        nc.sync.dma_start(out, bank[:])
